import numpy as np
import ml_dtypes


def mxq(x, axis, fmt="e4m3"):
    dtype, down = {"e4m3": (ml_dtypes.float8_e4m3fn, 7), "e5m2": (ml_dtypes.float8_e5m2, 14)}[fmt]
    v = np.moveaxis(np.asarray(x, np.float32).astype(ml_dtypes.bfloat16).astype(np.float64), axis, -1)
    blocks = v.reshape(v.shape[:-1] + (-1, 32))
    amax = np.abs(blocks).max(-1, keepdims=True)
    byte = np.maximum(np.where(amax > 0, np.frexp(amax)[1] - 1 + 127, 0) - down, 1)
    scale = np.exp2(byte - 127.0)
    codes = (blocks / scale).astype(np.float32).astype(dtype).astype(np.float64)
    return np.moveaxis((codes * scale).reshape(v.shape), -1, axis)


WIDE = False


def mx_kscale(k):
    if not WIDE:
        return np.ones(k)
    levels = np.array([10, -10, 5, -5, 0])
    if k % 512:
        return np.exp2(np.random.permutation(np.resize(levels, k // 32))).repeat(32)
    a = np.empty((k // 512, 16))
    for p in range(k // 512):
        a[p, :8] = np.random.permutation(np.resize(levels, 8))
        for g in range(8):
            far = levels[np.abs(levels - a[p, g]) >= 10]
            a[p, g + 8] = far[np.random.randint(len(far))]
    return np.exp2(a.ravel()).repeat(32)


BF16 = ml_dtypes.bfloat16


def bf(x):
    return np.asarray(x, np.float32).astype(BF16)


def f64(x):
    return np.asarray(x).astype(np.float64)


E2M1 = np.array([0.0, 0.5, 1.0, 1.5, 2.0, 3.0, 4.0, 6.0, -0.0, -0.5, -1.0, -1.5, -2.0, -3.0, -4.0, -6.0])


def pack_weight(w, fmt):
    k, n = w.shape
    w = f64(bf(w)).reshape(k // 32, 32, n)
    amax = np.abs(w).max(1)
    if fmt == "e4m3":
        byte = np.frexp(amax)[1] - 1 + 127 - 7
    else:
        mant, ex = np.frexp(amax / 6.0)
        byte = np.where(mant > 0.5, ex, ex - 1) + 127
    byte = np.clip(np.where(amax > 0, byte, 1), 1, 254)
    scaled = (w * np.exp2(127.0 - byte)[:, None, :]).reshape(k, n).astype(np.float32)
    by_word = np.ascontiguousarray(scaled.reshape(k // 512, 128, 4, n).transpose(0, 1, 3, 2))
    if fmt == "e4m3":
        words = by_word.astype(ml_dtypes.float8_e4m3fn).view(np.uint8)
    else:
        c = by_word.astype(ml_dtypes.float4_e2m1fn).view(np.uint8) & 0xF
        words = c[..., 0::2] | (c[..., 1::2] << 4)
    return np.ascontiguousarray(words), np.ascontiguousarray(byte.astype(np.uint8).reshape(k // 512, 16, n))


def unpack_weight(words, scales, fmt):
    g, p, n, _ = words.shape
    if fmt == "e4m3":
        vals = np.ascontiguousarray(words).view(ml_dtypes.float8_e4m3fn).astype(np.float64)
    else:
        nib = np.empty((g, p, n, 4), np.uint8)
        nib[..., 0::2] = words & 0xF
        nib[..., 1::2] = words >> 4
        vals = E2M1[nib]
    vals = vals * np.repeat(np.exp2(scales.astype(np.float64) - 127.0), 8, axis=1)[..., None]
    return vals.transpose(0, 1, 3, 2).reshape(g * 512, n)


IN, H, C, B = 1024, 1024, 2, 512
QH = H % 512 == 0


def sigmoid(v):
    return 1.0 / (1.0 + np.exp(-v))


def setup_inputs():
    s = mx_kscale(IN)
    t = mx_kscale(H) if QH else np.ones(H)
    input_word = bf(np.random.standard_normal((B, IN)) * s)
    hidden_states = bf(np.random.standard_normal((B, H)) * t)
    wx = np.random.uniform(-1.0, 1.0, (C, 2 * H, IN)) / np.sqrt(IN) / s
    cat = np.ascontiguousarray(wx.swapaxes(1, 2)).reshape(-1, 2 * H)
    words, scales = pack_weight(cat, "e4m3")
    bx = bf(np.random.standard_normal((C, 2 * H)) * 0.3)
    Wh = bf(np.random.uniform(-1.0, 1.0, (C, 2 * H, H)) / np.sqrt(H) / t)
    return {"input_word": input_word,
            "hidden_states": hidden_states,
            "Wx_words": words,
            "Wx_scales": scales,
            "bx": bx,
            "Wh": Wh}


def reference(input_word, hidden_states, Wx_words, Wx_scales, bx, Wh):
    px = mxq(f64(input_word), 1, "e4m3") @ unpack_weight(Wx_words, Wx_scales, "e4m3").reshape(C, IN, 2 * H)
    if QH:
        ph = mxq(f64(hidden_states), 1, "e4m3") @ mxq(f64(Wh), 2, "e4m3").transpose(0, 2, 1)
    else:
        ph = f64(hidden_states) @ f64(Wh).transpose(0, 2, 1)
    net = px.transpose(1, 0, 2) + ph.transpose(1, 0, 2) + f64(bx)[None, :, :]
    input_gate, cell_states = net[..., :H], net[..., H:]
    cell_input = np.tanh(cell_states)
    input_gate = sigmoid(input_gate)
    return (cell_input, input_gate)

@@ -1,0 +1,234 @@
+from contextlib import ExitStack
+
+import concourse.mybir as mybir
+from concourse.masks import make_identity
+
+F32 = mybir.dt.float32
+BF16 = mybir.dt.bfloat16
+I32 = mybir.dt.int32
+U32 = mybir.dt.uint32
+U8 = mybir.dt.uint8
+FP8X4 = mybir.dt.float8_e4m3fn_x4
+ACT = mybir.ActivationFunctionType
+
+P = 128
+PACK = 4
+PAIR = 2
+K_PASS = P * PACK
+BATCH = 512
+K = 1024
+HID = 1024
+CELLS = 2
+PASSES = K // K_PASS
+PASS_WORDS = K_PASS // PAIR
+B_TILES = BATCH // P
+CHUNK = 512
+SLABS = HID // CHUNK
+ROWS = CHUNK // P
+RESULT_BUFS = 20
+
+FLOPS = 2 * BATCH * (CELLS * 2 * HID) * (2 * K)
+
+
+def tile_compute_gate_e_kernel(tc, input_word, hidden_states, Wx_words, Wx_scales, bx, Wh, out_0, out_1):
+    nc = tc.nc
+
+    chunks = []
+    for func, out, first_n in ((ACT.Sigmoid, out_1, 0), (ACT.Tanh, out_0, HID)):
+        for cell in range(CELLS):
+            for slab in range(SLABS):
+                chunks.append((func, out, cell, slab * CHUNK, first_n + slab * CHUNK))
+    n_chunks = len(chunks)
+
+    with ExitStack() as ctx:
+        keep = ctx.enter_context(tc.tile_pool(name="keep", bufs=1))
+        act_stage = ctx.enter_context(tc.tile_pool(name="act_stage", bufs=3))
+        wh_stage = ctx.enter_context(tc.tile_pool(name="wh_stage", bufs=2))
+        results = ctx.enter_context(tc.tile_pool(name="results", bufs=RESULT_BUFS))
+        flip_banks = ctx.enter_context(tc.psum_pool(name="flip_banks", bufs=4))
+        sum_banks = ctx.enter_context(tc.psum_pool(name="sum_banks", bufs=B_TILES))
+        ctx.enter_context(tc.manual_schedule())
+
+        wx_planes = keep.tile([P, 2 * HID], U8, name="wx_planes", align_bytes=64)
+        nc.vector.memset(wx_planes[:].bitcast(I32), 0)
+        bias_rows = keep.tile([P, CHUNK], BF16, name="bias_rows")
+        nc.vector.memset(bias_rows[:], 0.0)
+        warm = keep.tile([P, 1], F32, name="warm")
+        nc.vector.memset(warm[:], 0.0)
+        nc.scalar.activation(out=warm[:], in_=warm[:], func=ACT.Sigmoid)
+        ident_f32 = keep.tile([P, P], F32, name="ident_f32")
+        make_identity(nc, ident_f32[:])
+        ident_bf16 = keep.tile([P, P], BF16, name="ident_bf16")
+        make_identity(nc, ident_bf16[:])
+
+        def load_activations(rows, name):
+            halves = []
+            for half in range(B_TILES // 2):
+                raw = keep.tile([P, 2, K], BF16, name="%s_raw%d" % (name, half))
+                nc.sync.dma_start(
+                    out=raw[:],
+                    in_=rows[2 * P * half : 2 * P * (half + 1), :].rearrange("(t p) k -> p t k", p=P),
+                )
+                halves.append(raw)
+            return halves
+
+        def load_wx(j):
+            cell, n0 = chunks[j][2], chunks[j][4]
+            words = keep.tile([P, PASSES, CHUNK], U32, name="wx_words%d" % j, align_bytes=64)
+            nc.sync.dma_start(
+                out=words[:].bitcast(I32),
+                in_=Wx_words[PASSES * cell : PASSES * (cell + 1), :, n0 : n0 + CHUNK, :]
+                .rearrange("g p n t -> p g (n t)")
+                .bitcast(I32),
+            )
+            return words
+
+        def load_wh(j):
+            cell, n0 = chunks[j][2], chunks[j][4]
+            raw = keep.tile([P, ROWS, K], BF16, name="wh_raw%d" % j)
+            rows = Wh[cell, n0 : n0 + CHUNK, :].rearrange("(q r) k -> q r k", r=ROWS)
+            for first in range(0, ROWS, PAIR):
+                nc.sync.dma_start(out=raw[:, first : first + PAIR, :], in_=rows[:, first : first + PAIR, :])
+            return raw
+
+        x_raw = load_activations(input_word, "x")
+        for quadrant in range(4):
+            nc.sync.dma_start(
+                out=wx_planes[32 * quadrant : 32 * quadrant + 16, :].bitcast(I32),
+                in_=Wx_scales[:, 4 * quadrant : 4 * quadrant + 4, :].bitcast(I32),
+            )
+        nc.sync.dma_start(out=bias_rows[0 : CELLS * 2 * SLABS, :], in_=bx.rearrange("c (s n) -> (c s) n", n=CHUNK))
+        wx_words = [load_wx(0)]
+        h_raw = load_activations(hidden_states, "h")
+        wh_raw = [load_wh(0), load_wh(1)]
+        for j in range(1, n_chunks):
+            if j + 1 < n_chunks:
+                wh_raw.append(load_wh(j + 1))
+            wx_words.append(load_wx(j))
+
+        def word_columns(g, u):
+            return slice(PASS_WORDS * g + u, PASS_WORDS * (g + 1), PAIR)
+
+        def quantise_activations(raw_halves, name):
+            codes = keep.tile([P, B_TILES, PASSES * P], U32, name="%s_codes" % name, align_bytes=64)
+            planes = keep.tile([P, B_TILES, PASSES * P], U8, name="%s_planes" % name, align_bytes=64)
+            for bt in range(B_TILES):
+                words = raw_halves[bt // 2][:, bt % 2, :].bitcast(F32)
+                flipped = flip_banks.tile([P, PASSES, PAIR, P], F32, name="flipped", tag="bank")
+                for g in range(PASSES):
+                    for u in range(PAIR):
+                        nc.tensor.transpose(flipped[:, g, u, :], words[:, word_columns(g, u)], ident_f32[:])
+                grouped = act_stage.tile([P, PASSES, P, PACK], BF16, name="grouped", align_bytes=64)
+                copy = nc.scalar.copy if bt % 2 == 0 else nc.vector.tensor_copy
+                copy(out=grouped[:].bitcast(F32), in_=flipped[:].rearrange("p g u b -> p g b u"))
+                nc.vector.quantize_mx(
+                    out=codes[:, bt, :].bitcast(FP8X4),
+                    scales=planes[:, bt, :],
+                    in_=grouped[:].rearrange("p g b t -> p (g b t)"),
+                )
+            return codes, planes
+
+        bias_all = keep.tile([P, CELLS * 2 * SLABS, CHUNK], BF16, name="bias_all")
+
+        def spread_bias(first_row):
+            spread = flip_banks.tile([P, PAIR, CHUNK], BF16, name="spread", tag="bank")
+            for i in range(PAIR):
+                row = first_row + i
+                nc.tensor.matmul(
+                    spread[:, i, :],
+                    lhsT=ident_bf16[:, row : row + 1].to_broadcast([P, P]),
+                    rhs=bias_rows[:],
+                    start=True,
+                    stop=True,
+                )
+            nc.vector.tensor_copy(out=bias_all[:, first_row : first_row + PAIR, :], in_=spread[:])
+
+        def transpose_wh(j):
+            words = wh_raw[j][:].bitcast(F32)
+            grouped = wh_stage.tile([P, PASSES, CHUNK, PACK], BF16, name="wh_grouped", align_bytes=64)
+            for first in range(0, ROWS, PAIR):
+                for g in range(PASSES):
+                    flipped = flip_banks.tile([P, PAIR, PAIR, P], F32, name="flipped", tag="bank")
+                    for r in range(PAIR):
+                        for u in range(PAIR):
+                            nc.tensor.transpose(
+                                flipped[:, r, u, :], words[:, first + r, word_columns(g, u)], ident_f32[:]
+                            )
+                    nc.scalar.copy(
+                        out=grouped[:, g].bitcast(F32).rearrange("p (q r) u -> p q r u", r=ROWS)[
+                            :, :, first : first + PAIR, :
+                        ],
+                        in_=flipped[:].rearrange("p r u q -> p q r u"),
+                    )
+            return grouped
+
+        def quantise_wh(grouped):
+            codes = wh_stage.tile([P, PASSES, CHUNK], U32, name="wh_codes", align_bytes=64)
+            planes = wh_stage.tile([P, PASSES, CHUNK], U8, name="wh_planes", align_bytes=64)
+            for g in range(PASSES):
+                nc.vector.quantize_mx(
+                    out=codes[:, g, :].bitcast(FP8X4),
+                    scales=planes[:, g, :],
+                    in_=grouped[:, g].rearrange("p n t -> p (n t)"),
+                )
+            return codes, planes
+
+        def open_sums(j):
+            cell, n0 = chunks[j][2], chunks[j][4]
+            sums = []
+            for bt in range(B_TILES):
+                bank = sum_banks.tile([P, CHUNK], F32, name="sums")
+                for g in range(PASSES):
+                    nc.tensor.matmul_mx(
+                        out=bank[:],
+                        lhsT=x_codes[:, bt, P * g : P * (g + 1)].bitcast(FP8X4),
+                        lhsT_scale=x_planes[:, bt, P * g : P * (g + 1)],
+                        rhs=wx_words[j][:, g, :].bitcast(FP8X4),
+                        rhs_scale=wx_planes[4 * (PASSES * cell + g) : P, n0 : n0 + CHUNK],
+                        start=(g == 0),
+                        stop=False,
+                    )
+                sums.append(bank)
+            return sums
+
+        def close_sums(j, sums, codes, planes):
+            func, out, cell, out_col, n0 = chunks[j]
+            for bt in range(B_TILES):
+                for g in range(PASSES):
+                    nc.tensor.matmul_mx(
+                        out=sums[bt][:],
+                        lhsT=h_codes[:, bt, P * g : P * (g + 1)].bitcast(FP8X4),
+                        lhsT_scale=h_planes[:, bt, P * g : P * (g + 1)],
+                        rhs=codes[:, g, :].bitcast(FP8X4),
+                        rhs_scale=planes[:, g, :],
+                        start=False,
+                        stop=(g == PASSES - 1),
+                    )
+            for bt in range(B_TILES):
+                result = results.tile([P, CHUNK], F32, name="result")
+                nc.vector.tensor_tensor(
+                    out=result[:],
+                    in0=sums[bt][:],
+                    in1=bias_all[:, 2 * SLABS * cell + n0 // CHUNK, :],
+                    op=mybir.AluOpType.add,
+                )
+                nc.scalar.activation(out=result[:], in_=result[:], func=func)
+                nc.sync.dma_start(out=out[P * bt : P * (bt + 1), cell, out_col : out_col + CHUNK], in_=result[:])
+
+        x_codes, x_planes = quantise_activations(x_raw, "x")
+        for cell in range(CELLS):
+            spread_bias(2 * SLABS * cell)
+        sums = open_sums(0)
+        h_codes, h_planes = quantise_activations(h_raw, "h")
+        codes, planes = quantise_wh(transpose_wh(0))
+        for cell in range(CELLS):
+            spread_bias(2 * SLABS * cell + SLABS)
+        wh_grouped = {1: transpose_wh(1)}
+        for j in range(n_chunks):
+            close_sums(j, sums, codes, planes)
+            if j + 1 < n_chunks:
+                codes, planes = quantise_wh(wh_grouped[j + 1])
+            if j + 2 < n_chunks:
+                wh_grouped[j + 2] = transpose_wh(j + 2)
+            if j + 1 < n_chunks:
+                sums = open_sums(j + 1)

@@ -143,8 +143,17 @@ def tile_compute_gate_e_kernel(tc, input_word, hidden_states, Wx_words, Wx_scale
                 )
             nc.vector.tensor_copy(out=bias_all[:, first_row : first_row + PAIR, :], in_=spread[:])
 
-        def transpose_wh(j):
-            words = wh_raw[j][:].bitcast(F32)
+        def sort_wh(j):
+            raw = wh_raw[j][:].bitcast(F32)
+            ordered = wh_stage.tile([P, ROWS, PASSES, PAIR, P], F32, name="wh_ordered")
+            for first in range(0, ROWS, PAIR):
+                nc.vector.tensor_copy(
+                    out=ordered[:, first : first + PAIR].rearrange("p r g u w -> p (r g) u w"),
+                    in_=raw[:, first : first + PAIR, :].rearrange("p r (g w u) -> p (r g) u w", g=PASSES, u=PAIR),
+                )
+            return ordered
+
+        def transpose_wh(ordered):
             grouped = wh_stage.tile([P, PASSES, CHUNK, PACK], BF16, name="wh_grouped", align_bytes=64)
             for first in range(0, ROWS, PAIR):
                 for g in range(PASSES):
@@ -152,7 +161,7 @@ def tile_compute_gate_e_kernel(tc, input_word, hidden_states, Wx_words, Wx_scale
                     for r in range(PAIR):
                         for u in range(PAIR):
                             nc.tensor.transpose(
-                                flipped[:, r, u, :], words[:, first + r, word_columns(g, u)], ident_f32[:]
+                                flipped[:, r, u, :], ordered[:, first + r, g, u, :], ident_f32[:]
                             )
                     nc.scalar.copy(
                         out=grouped[:, g].bitcast(F32).rearrange("p (q r) u -> p q r u", r=ROWS)[
@@ -220,15 +229,20 @@ def tile_compute_gate_e_kernel(tc, input_word, hidden_states, Wx_words, Wx_scale
             spread_bias(2 * SLABS * cell)
         sums = open_sums(0)
         h_codes, h_planes = quantise_activations(h_raw, "h")
-        codes, planes = quantise_wh(transpose_wh(0))
+        grouped = transpose_wh(sort_wh(0))
+        wh_ordered = {1: sort_wh(1)}
+        codes, planes = quantise_wh(grouped)
         for cell in range(CELLS):
             spread_bias(2 * SLABS * cell + SLABS)
-        wh_grouped = {1: transpose_wh(1)}
+        wh_grouped = {1: transpose_wh(wh_ordered[1])}
+        wh_ordered[2] = sort_wh(2)
         for j in range(n_chunks):
             close_sums(j, sums, codes, planes)
             if j + 1 < n_chunks:
                 codes, planes = quantise_wh(wh_grouped[j + 1])
             if j + 2 < n_chunks:
-                wh_grouped[j + 2] = transpose_wh(j + 2)
+                wh_grouped[j + 2] = transpose_wh(wh_ordered[j + 2])
+            if j + 3 < n_chunks:
+                wh_ordered[j + 3] = sort_wh(j + 3)
             if j + 1 < n_chunks:
                 sums = open_sums(j + 1)

@@ -42,7 +42,6 @@ def tile_compute_gate_e_kernel(tc, input_word, hidden_states, Wx_words, Wx_scale
 
     with ExitStack() as ctx:
         keep = ctx.enter_context(tc.tile_pool(name="keep", bufs=1))
-        act_stage = ctx.enter_context(tc.tile_pool(name="act_stage", bufs=3))
         wh_stage = ctx.enter_context(tc.tile_pool(name="wh_stage", bufs=2))
         results = ctx.enter_context(tc.tile_pool(name="results", bufs=RESULT_BUFS))
         flip_banks = ctx.enter_context(tc.psum_pool(name="flip_banks", bufs=4))
@@ -51,26 +50,19 @@ def tile_compute_gate_e_kernel(tc, input_word, hidden_states, Wx_words, Wx_scale
 
         wx_planes = keep.tile([P, 2 * HID], U8, name="wx_planes", align_bytes=64)
         nc.vector.memset(wx_planes[:].bitcast(I32), 0)
-        bias_rows = keep.tile([P, CHUNK], BF16, name="bias_rows")
-        nc.vector.memset(bias_rows[:], 0.0)
         warm = keep.tile([P, 1], F32, name="warm")
         nc.vector.memset(warm[:], 0.0)
         nc.scalar.activation(out=warm[:], in_=warm[:], func=ACT.Sigmoid)
         ident_f32 = keep.tile([P, P], F32, name="ident_f32")
         make_identity(nc, ident_f32[:])
-        ident_bf16 = keep.tile([P, P], BF16, name="ident_bf16")
-        make_identity(nc, ident_bf16[:])
 
         def load_activations(rows, name):
-            halves = []
-            for half in range(B_TILES // 2):
-                raw = keep.tile([P, 2, K], BF16, name="%s_raw%d" % (name, half))
-                nc.sync.dma_start(
-                    out=raw[:],
-                    in_=rows[2 * P * half : 2 * P * (half + 1), :].rearrange("(t p) k -> p t k", p=P),
-                )
-                halves.append(raw)
-            return halves
+            tiles = []
+            for bt in range(B_TILES):
+                raw = keep.tile([P, K], BF16, name="%s_raw%d" % (name, bt))
+                nc.sync.dma_start(out=raw[:], in_=rows[P * bt : P * (bt + 1), :])
+                tiles.append(raw)
+            return tiles
 
         def load_wx(j):
             cell, n0 = chunks[j][2], chunks[j][4]
@@ -97,51 +89,44 @@ def tile_compute_gate_e_kernel(tc, input_word, hidden_states, Wx_words, Wx_scale
                 out=wx_planes[32 * quadrant : 32 * quadrant + 16, :].bitcast(I32),
                 in_=Wx_scales[:, 4 * quadrant : 4 * quadrant + 4, :].bitcast(I32),
             )
-        nc.sync.dma_start(out=bias_rows[0 : CELLS * 2 * SLABS, :], in_=bx.rearrange("c (s n) -> (c s) n", n=CHUNK))
         wx_words = [load_wx(0)]
+        wh_raw = [load_wh(0)]
         h_raw = load_activations(hidden_states, "h")
-        wh_raw = [load_wh(0), load_wh(1)]
-        for j in range(1, n_chunks):
-            if j + 1 < n_chunks:
-                wh_raw.append(load_wh(j + 1))
+        wh_raw.append(load_wh(1))
+        bias_all = keep.tile([P, CELLS, 2 * HID], BF16, name="bias_all")
+        nc.sync.dma_start(out=bias_all[:, :, 0:HID], in_=bx[:, 0:HID].partition_broadcast(P))
+        wx_words.append(load_wx(1))
+        for j in range(2, n_chunks):
+            wh_raw.append(load_wh(j))
             wx_words.append(load_wx(j))
+        nc.sync.dma_start(out=bias_all[:, :, HID : 2 * HID], in_=bx[:, HID : 2 * HID].partition_broadcast(P))
 
         def word_columns(g, u):
             return slice(PASS_WORDS * g + u, PASS_WORDS * (g + 1), PAIR)
 
-        def quantise_activations(raw_halves, name):
-            codes = keep.tile([P, B_TILES, PASSES * P], U32, name="%s_codes" % name, align_bytes=64)
-            planes = keep.tile([P, B_TILES, PASSES * P], U8, name="%s_planes" % name, align_bytes=64)
+        def transpose_activations(raw, name, copies):
+            staged = []
             for bt in range(B_TILES):
-                words = raw_halves[bt // 2][:, bt % 2, :].bitcast(F32)
+                words = raw[bt][:].bitcast(F32)
                 flipped = flip_banks.tile([P, PASSES, PAIR, P], F32, name="flipped", tag="bank")
                 for g in range(PASSES):
                     for u in range(PAIR):
                         nc.tensor.transpose(flipped[:, g, u, :], words[:, word_columns(g, u)], ident_f32[:])
-                grouped = act_stage.tile([P, PASSES, P, PACK], BF16, name="grouped", align_bytes=64)
-                copy = nc.scalar.copy if bt % 2 == 0 else nc.vector.tensor_copy
-                copy(out=grouped[:].bitcast(F32), in_=flipped[:].rearrange("p g u b -> p g b u"))
+                grouped = keep.tile([P, PASSES, P, PACK], BF16, name="%s_grouped%d" % (name, bt), align_bytes=64)
+                copies[bt](out=grouped[:].bitcast(F32), in_=flipped[:].rearrange("p g u b -> p g b u"))
+                staged.append(grouped)
+            return staged
+
+        def quantise_activations(staged, name):
+            codes = keep.tile([P, B_TILES, PASSES * P], U32, name="%s_codes" % name, align_bytes=64)
+            planes = keep.tile([P, B_TILES, PASSES * P], U8, name="%s_planes" % name, align_bytes=64)
+            for bt in range(B_TILES):
                 nc.vector.quantize_mx(
                     out=codes[:, bt, :].bitcast(FP8X4),
                     scales=planes[:, bt, :],
-                    in_=grouped[:].rearrange("p g b t -> p (g b t)"),
+                    in_=staged[bt][:].rearrange("p g b t -> p (g b t)"),
                 )
             return codes, planes
-
-        bias_all = keep.tile([P, CELLS * 2 * SLABS, CHUNK], BF16, name="bias_all")
-
-        def spread_bias(first_row):
-            spread = flip_banks.tile([P, PAIR, CHUNK], BF16, name="spread", tag="bank")
-            for i in range(PAIR):
-                row = first_row + i
-                nc.tensor.matmul(
-                    spread[:, i, :],
-                    lhsT=ident_bf16[:, row : row + 1].to_broadcast([P, P]),
-                    rhs=bias_rows[:],
-                    start=True,
-                    stop=True,
-                )
-            nc.vector.tensor_copy(out=bias_all[:, first_row : first_row + PAIR, :], in_=spread[:])
 
         def sort_wh(j):
             raw = wh_raw[j][:].bitcast(F32)
@@ -151,19 +136,22 @@ def tile_compute_gate_e_kernel(tc, input_word, hidden_states, Wx_words, Wx_scale
                     out=ordered[:, first : first + PAIR].rearrange("p r g u w -> p (r g) u w"),
                     in_=raw[:, first : first + PAIR, :].rearrange("p r (g w u) -> p (r g) u w", g=PASSES, u=PAIR),
                 )
-            return ordered
+            return lambda r, g, u: ordered[:, r, g, u, :]
 
-        def transpose_wh(ordered):
+        def unsorted_wh(j):
+            raw = wh_raw[j][:].bitcast(F32)
+            return lambda r, g, u: raw[:, r, word_columns(g, u)]
+
+        def transpose_wh(words, copies):
             grouped = wh_stage.tile([P, PASSES, CHUNK, PACK], BF16, name="wh_grouped", align_bytes=64)
+            copies = list(copies)
             for first in range(0, ROWS, PAIR):
                 for g in range(PASSES):
                     flipped = flip_banks.tile([P, PAIR, PAIR, P], F32, name="flipped", tag="bank")
                     for r in range(PAIR):
                         for u in range(PAIR):
-                            nc.tensor.transpose(
-                                flipped[:, r, u, :], ordered[:, first + r, g, u, :], ident_f32[:]
-                            )
-                    nc.scalar.copy(
+                            nc.tensor.transpose(flipped[:, r, u, :], words(first + r, g, u), ident_f32[:])
+                    copies.pop(0)(
                         out=grouped[:, g].bitcast(F32).rearrange("p (q r) u -> p q r u", r=ROWS)[
                             :, :, first : first + PAIR, :
                         ],
@@ -218,30 +206,35 @@ def tile_compute_gate_e_kernel(tc, input_word, hidden_states, Wx_words, Wx_scale
                 nc.vector.tensor_tensor(
                     out=result[:],
                     in0=sums[bt][:],
-                    in1=bias_all[:, 2 * SLABS * cell + n0 // CHUNK, :],
+                    in1=bias_all[:, cell, n0 : n0 + CHUNK],
                     op=mybir.AluOpType.add,
                 )
                 nc.scalar.activation(out=result[:], in_=result[:], func=func)
                 nc.sync.dma_start(out=out[P * bt : P * (bt + 1), cell, out_col : out_col + CHUNK], in_=result[:])
 
-        x_codes, x_planes = quantise_activations(x_raw, "x")
-        for cell in range(CELLS):
-            spread_bias(2 * SLABS * cell)
+        on_scalar, on_vector = nc.scalar.copy, nc.vector.tensor_copy
+        x_codes, x_planes = quantise_activations(
+            transpose_activations(x_raw, "x", (on_scalar, on_vector, on_scalar, on_scalar)), "x"
+        )
+        ordered = sort_wh(0)
         sums = open_sums(0)
-        h_codes, h_planes = quantise_activations(h_raw, "h")
-        grouped = transpose_wh(sort_wh(0))
-        wh_ordered = {1: sort_wh(1)}
-        codes, planes = quantise_wh(grouped)
-        for cell in range(CELLS):
-            spread_bias(2 * SLABS * cell + SLABS)
-        wh_grouped = {1: transpose_wh(wh_ordered[1])}
-        wh_ordered[2] = sort_wh(2)
-        for j in range(n_chunks):
+        wh_grouped = {0: transpose_wh(ordered, (on_scalar, on_vector) * 2)}
+        h_staged = transpose_activations(h_raw, "h", (on_scalar,) * 4)
+        codes, planes = quantise_wh(wh_grouped[0])
+        h_codes, h_planes = quantise_activations(h_staged, "h")
+        wh_ordered = {}
+        close_sums(0, sums, codes, planes)
+        wh_grouped[1] = transpose_wh(unsorted_wh(1), (on_vector, on_scalar) * 2)
+        codes, planes = quantise_wh(wh_grouped[1])
+        sums = open_sums(1)
+        wh_grouped[2] = transpose_wh(unsorted_wh(2), (on_scalar,) * 4)
+        wh_ordered[3] = sort_wh(3)
+        for j in range(1, n_chunks):
             close_sums(j, sums, codes, planes)
             if j + 1 < n_chunks:
                 codes, planes = quantise_wh(wh_grouped[j + 1])
             if j + 2 < n_chunks:
-                wh_grouped[j + 2] = transpose_wh(wh_ordered[j + 2])
+                wh_grouped[j + 2] = transpose_wh(wh_ordered[j + 2], (on_scalar,) * 4)
             if j + 3 < n_chunks:
                 wh_ordered[j + 3] = sort_wh(j + 3)
             if j + 1 < n_chunks:

@@ -25,6 +25,9 @@ B_TILES = BATCH // P
 CHUNK = 512
 SLABS = HID // CHUNK
 ROWS = CHUNK // P
+ALL_COLS = slice(0, CHUNK)
+END_PIECES = (slice(0, 256), slice(256, 384), slice(384, 512))
+BIAS_BEHIND = 3
 RESULT_BUFS = 20
 
 FLOPS = 2 * BATCH * (CELLS * 2 * HID) * (2 * K)
@@ -53,8 +56,12 @@ def tile_compute_gate_e_kernel(tc, input_word, hidden_states, Wx_words, Wx_scale
         warm = keep.tile([P, 1], F32, name="warm")
         nc.vector.memset(warm[:], 0.0)
         nc.scalar.activation(out=warm[:], in_=warm[:], func=ACT.Sigmoid)
+        bias_rows = keep.tile([P, CHUNK], BF16, name="bias_rows")
+        nc.vector.memset(bias_rows[:], 0.0)
+        ident_bf16 = keep.tile([P, P], BF16, name="ident_bf16")
         ident_f32 = keep.tile([P, P], F32, name="ident_f32")
         make_identity(nc, ident_f32[:])
+        make_identity(nc, ident_bf16[:])
 
         def load_activations(rows, name):
             tiles = []
@@ -83,22 +90,22 @@ def tile_compute_gate_e_kernel(tc, input_word, hidden_states, Wx_words, Wx_scale
                 nc.sync.dma_start(out=raw[:, first : first + PAIR, :], in_=rows[:, first : first + PAIR, :])
             return raw
 
+        bias_all = keep.tile([P, CELLS, 2 * HID], BF16, name="bias_all")
         x_raw = load_activations(input_word, "x")
         for quadrant in range(4):
             nc.sync.dma_start(
                 out=wx_planes[32 * quadrant : 32 * quadrant + 16, :].bitcast(I32),
                 in_=Wx_scales[:, 4 * quadrant : 4 * quadrant + 4, :].bitcast(I32),
             )
+        nc.sync.dma_start(out=bias_rows[0:SLABS, :], in_=bx[0, 0:HID].rearrange("(s n) -> s n", n=CHUNK))
         wx_words = [load_wx(0)]
         wh_raw = [load_wh(0)]
         h_raw = load_activations(hidden_states, "h")
-        wh_raw.append(load_wh(1))
-        bias_all = keep.tile([P, CELLS, 2 * HID], BF16, name="bias_all")
-        nc.sync.dma_start(out=bias_all[:, :, 0:HID], in_=bx[:, 0:HID].partition_broadcast(P))
-        wx_words.append(load_wx(1))
-        for j in range(2, n_chunks):
+        for j in range(1, n_chunks):
             wh_raw.append(load_wh(j))
             wx_words.append(load_wx(j))
+            if j == BIAS_BEHIND:
+                nc.sync.dma_start(out=bias_all[:, 1, 0:HID], in_=bx[1, 0:HID].partition_broadcast(P))
         nc.sync.dma_start(out=bias_all[:, :, HID : 2 * HID], in_=bx[:, HID : 2 * HID].partition_broadcast(P))
 
         def word_columns(g, u):
@@ -170,63 +177,88 @@ def tile_compute_gate_e_kernel(tc, input_word, hidden_states, Wx_words, Wx_scale
                 )
             return codes, planes
 
-        def open_sums(j):
+        def spread_bias():
+            spread = flip_banks.tile([P, SLABS, CHUNK], BF16, name="spread", tag="bank")
+            for row in range(SLABS):
+                nc.tensor.matmul(
+                    spread[:, row, :],
+                    lhsT=ident_bf16[:, row : row + 1].to_broadcast([P, P]),
+                    rhs=bias_rows[:],
+                    start=True,
+                    stop=True,
+                )
+            nc.scalar.copy(out=bias_all[:, 0, 0:HID].rearrange("p (s n) -> p s n", n=CHUNK), in_=spread[:])
+
+        def input_passes(bank, j, bt, cols):
             cell, n0 = chunks[j][2], chunks[j][4]
+            for g in range(PASSES):
+                nc.tensor.matmul_mx(
+                    out=bank[:, cols],
+                    lhsT=x_codes[:, bt, P * g : P * (g + 1)].bitcast(FP8X4),
+                    lhsT_scale=x_planes[:, bt, P * g : P * (g + 1)],
+                    rhs=wx_words[j][:, g, cols].bitcast(FP8X4),
+                    rhs_scale=wx_planes[4 * (PASSES * cell + g) : P, n0 + cols.start : n0 + cols.stop],
+                    start=(g == 0),
+                    stop=False,
+                )
+
+        def hidden_passes(bank, bt, cols, codes, planes):
+            for g in range(PASSES):
+                nc.tensor.matmul_mx(
+                    out=bank[:, cols],
+                    lhsT=h_codes[:, bt, P * g : P * (g + 1)].bitcast(FP8X4),
+                    lhsT_scale=h_planes[:, bt, P * g : P * (g + 1)],
+                    rhs=codes[:, g, cols].bitcast(FP8X4),
+                    rhs_scale=planes[:, g, cols],
+                    start=False,
+                    stop=(g == PASSES - 1),
+                )
+
+        def finish(bank, j, bt, cols):
+            func, out, cell, out_col, n0 = chunks[j]
+            width = cols.stop - cols.start
+            result = results.tile([P, width], F32, name="result")
+            nc.vector.tensor_tensor(
+                out=result[:],
+                in0=bank[:, cols],
+                in1=bias_all[:, cell, n0 + cols.start : n0 + cols.stop],
+                op=mybir.AluOpType.add,
+            )
+            nc.scalar.activation(out=result[:], in_=result[:], func=func)
+            nc.sync.dma_start(
+                out=out[P * bt : P * (bt + 1), cell, out_col + cols.start : out_col + cols.stop], in_=result[:]
+            )
+
+        def open_sums(j, batch_tiles):
             sums = []
-            for bt in range(B_TILES):
+            for bt in batch_tiles:
                 bank = sum_banks.tile([P, CHUNK], F32, name="sums")
-                for g in range(PASSES):
-                    nc.tensor.matmul_mx(
-                        out=bank[:],
-                        lhsT=x_codes[:, bt, P * g : P * (g + 1)].bitcast(FP8X4),
-                        lhsT_scale=x_planes[:, bt, P * g : P * (g + 1)],
-                        rhs=wx_words[j][:, g, :].bitcast(FP8X4),
-                        rhs_scale=wx_planes[4 * (PASSES * cell + g) : P, n0 : n0 + CHUNK],
-                        start=(g == 0),
-                        stop=False,
-                    )
+                input_passes(bank, j, bt, ALL_COLS)
                 sums.append(bank)
             return sums
 
         def close_sums(j, sums, codes, planes):
-            func, out, cell, out_col, n0 = chunks[j]
-            for bt in range(B_TILES):
-                for g in range(PASSES):
-                    nc.tensor.matmul_mx(
-                        out=sums[bt][:],
-                        lhsT=h_codes[:, bt, P * g : P * (g + 1)].bitcast(FP8X4),
-                        lhsT_scale=h_planes[:, bt, P * g : P * (g + 1)],
-                        rhs=codes[:, g, :].bitcast(FP8X4),
-                        rhs_scale=planes[:, g, :],
-                        start=False,
-                        stop=(g == PASSES - 1),
-                    )
-            for bt in range(B_TILES):
-                result = results.tile([P, CHUNK], F32, name="result")
-                nc.vector.tensor_tensor(
-                    out=result[:],
-                    in0=sums[bt][:],
-                    in1=bias_all[:, cell, n0 : n0 + CHUNK],
-                    op=mybir.AluOpType.add,
-                )
-                nc.scalar.activation(out=result[:], in_=result[:], func=func)
-                nc.sync.dma_start(out=out[P * bt : P * (bt + 1), cell, out_col : out_col + CHUNK], in_=result[:])
+            for bt, bank in enumerate(sums):
+                hidden_passes(bank, bt, ALL_COLS, codes, planes)
+            for bt, bank in enumerate(sums):
+                finish(bank, j, bt, ALL_COLS)
 
         on_scalar, on_vector = nc.scalar.copy, nc.vector.tensor_copy
         x_codes, x_planes = quantise_activations(
             transpose_activations(x_raw, "x", (on_scalar, on_vector, on_scalar, on_scalar)), "x"
         )
         ordered = sort_wh(0)
-        sums = open_sums(0)
+        sums = open_sums(0, range(B_TILES))
         wh_grouped = {0: transpose_wh(ordered, (on_scalar, on_vector) * 2)}
         h_staged = transpose_activations(h_raw, "h", (on_scalar,) * 4)
+        spread_bias()
         codes, planes = quantise_wh(wh_grouped[0])
         h_codes, h_planes = quantise_activations(h_staged, "h")
         wh_ordered = {}
         close_sums(0, sums, codes, planes)
         wh_grouped[1] = transpose_wh(unsorted_wh(1), (on_vector, on_scalar) * 2)
         codes, planes = quantise_wh(wh_grouped[1])
-        sums = open_sums(1)
+        sums = open_sums(1, range(B_TILES))
         wh_grouped[2] = transpose_wh(unsorted_wh(2), (on_scalar,) * 4)
         wh_ordered[3] = sort_wh(3)
         for j in range(1, n_chunks):
@@ -238,4 +270,9 @@ def tile_compute_gate_e_kernel(tc, input_word, hidden_states, Wx_words, Wx_scale
             if j + 3 < n_chunks:
                 wh_ordered[j + 3] = sort_wh(j + 3)
             if j + 1 < n_chunks:
-                sums = open_sums(j + 1)
+                sums = open_sums(j + 1, range(B_TILES if j + 2 < n_chunks else B_TILES - 1))
+        for cols in END_PIECES:
+            bank = flip_banks.tile([P, CHUNK], F32, name="end_sums", tag="bank")
+            input_passes(bank, n_chunks - 1, B_TILES - 1, cols)
+            hidden_passes(bank, B_TILES - 1, cols, codes, planes)
+            finish(bank, n_chunks - 1, B_TILES - 1, cols)

@@ -45,6 +45,8 @@ def tile_compute_gate_e_kernel(tc, input_word, hidden_states, Wx_words, Wx_scale
 
     with ExitStack() as ctx:
         keep = ctx.enter_context(tc.tile_pool(name="keep", bufs=1))
+        wh_rows = ctx.enter_context(tc.tile_pool(name="wh_rows", bufs=6))
+        wh_order = ctx.enter_context(tc.tile_pool(name="wh_order", bufs=3))
         wh_stage = ctx.enter_context(tc.tile_pool(name="wh_stage", bufs=2))
         results = ctx.enter_context(tc.tile_pool(name="results", bufs=RESULT_BUFS))
         flip_banks = ctx.enter_context(tc.psum_pool(name="flip_banks", bufs=4))
@@ -57,7 +59,7 @@ def tile_compute_gate_e_kernel(tc, input_word, hidden_states, Wx_words, Wx_scale
         nc.vector.memset(warm[:], 0.0)
         nc.scalar.activation(out=warm[:], in_=warm[:], func=ACT.Sigmoid)
         bias_rows = keep.tile([P, CHUNK], BF16, name="bias_rows")
-        nc.vector.memset(bias_rows[:], 0.0)
+        nc.vector.memset(bias_rows[:].bitcast(I32), 0)
         ident_bf16 = keep.tile([P, P], BF16, name="ident_bf16")
         ident_f32 = keep.tile([P, P], F32, name="ident_f32")
         make_identity(nc, ident_f32[:])
@@ -84,7 +86,7 @@ def tile_compute_gate_e_kernel(tc, input_word, hidden_states, Wx_words, Wx_scale
 
         def load_wh(j):
             cell, n0 = chunks[j][2], chunks[j][4]
-            raw = keep.tile([P, ROWS, K], BF16, name="wh_raw%d" % j)
+            raw = wh_rows.tile([P, ROWS, K], BF16, name="wh_raw")
             rows = Wh[cell, n0 : n0 + CHUNK, :].rearrange("(q r) k -> q r k", r=ROWS)
             for first in range(0, ROWS, PAIR):
                 nc.sync.dma_start(out=raw[:, first : first + PAIR, :], in_=rows[:, first : first + PAIR, :])
@@ -92,17 +94,21 @@ def tile_compute_gate_e_kernel(tc, input_word, hidden_states, Wx_words, Wx_scale
 
         bias_all = keep.tile([P, CELLS, 2 * HID], BF16, name="bias_all")
         x_raw = load_activations(input_word, "x")
+        nc.sync.dma_start(out=bias_rows[0:SLABS, :], in_=bx[0, 0:HID].rearrange("(s n) -> s n", n=CHUNK))
         for quadrant in range(4):
             nc.sync.dma_start(
                 out=wx_planes[32 * quadrant : 32 * quadrant + 16, :].bitcast(I32),
                 in_=Wx_scales[:, 4 * quadrant : 4 * quadrant + 4, :].bitcast(I32),
             )
-        nc.sync.dma_start(out=bias_rows[0:SLABS, :], in_=bx[0, 0:HID].rearrange("(s n) -> s n", n=CHUNK))
         wx_words = [load_wx(0)]
         wh_raw = [load_wh(0)]
         h_raw = load_activations(hidden_states, "h")
-        for j in range(1, n_chunks):
-            wh_raw.append(load_wh(j))
+        wh_raw.append(load_wh(1))
+        wx_words.append(load_wx(1))
+        wh_raw.append(load_wh(2))
+        for j in range(2, n_chunks):
+            if j + 1 < n_chunks:
+                wh_raw.append(load_wh(j + 1))
             wx_words.append(load_wx(j))
             if j == BIAS_BEHIND:
                 nc.sync.dma_start(out=bias_all[:, 1, 0:HID], in_=bx[1, 0:HID].partition_broadcast(P))
@@ -111,14 +117,24 @@ def tile_compute_gate_e_kernel(tc, input_word, hidden_states, Wx_words, Wx_scale
         def word_columns(g, u):
             return slice(PASS_WORDS * g + u, PASS_WORDS * (g + 1), PAIR)
 
-        def transpose_activations(raw, name, copies):
+        def sort_activations(raw, name):
+            ordered = keep.tile([P, PASSES, PAIR, P], F32, name=name)
+            nc.vector.tensor_copy(
+                out=ordered[:], in_=raw[:].bitcast(F32).rearrange("p (g w u) -> p g u w", g=PASSES, u=PAIR)
+            )
+            return lambda g, u: ordered[:, g, u, :]
+
+        def unsorted_activations(raw):
+            words = raw[:].bitcast(F32)
+            return lambda g, u: words[:, word_columns(g, u)]
+
+        def transpose_activations(words, name, copies):
             staged = []
             for bt in range(B_TILES):
-                words = raw[bt][:].bitcast(F32)
                 flipped = flip_banks.tile([P, PASSES, PAIR, P], F32, name="flipped", tag="bank")
                 for g in range(PASSES):
                     for u in range(PAIR):
-                        nc.tensor.transpose(flipped[:, g, u, :], words[:, word_columns(g, u)], ident_f32[:])
+                        nc.tensor.transpose(flipped[:, g, u, :], words[bt](g, u), ident_f32[:])
                 grouped = keep.tile([P, PASSES, P, PACK], BF16, name="%s_grouped%d" % (name, bt), align_bytes=64)
                 copies[bt](out=grouped[:].bitcast(F32), in_=flipped[:].rearrange("p g u b -> p g b u"))
                 staged.append(grouped)
@@ -135,19 +151,15 @@ def tile_compute_gate_e_kernel(tc, input_word, hidden_states, Wx_words, Wx_scale
                 )
             return codes, planes
 
-        def sort_wh(j):
+        def sort_wh(j, copy):
             raw = wh_raw[j][:].bitcast(F32)
-            ordered = wh_stage.tile([P, ROWS, PASSES, PAIR, P], F32, name="wh_ordered")
+            ordered = wh_order.tile([P, ROWS, PASSES, PAIR, P], F32, name="wh_ordered")
             for first in range(0, ROWS, PAIR):
-                nc.vector.tensor_copy(
+                copy(
                     out=ordered[:, first : first + PAIR].rearrange("p r g u w -> p (r g) u w"),
                     in_=raw[:, first : first + PAIR, :].rearrange("p r (g w u) -> p (r g) u w", g=PASSES, u=PAIR),
                 )
             return lambda r, g, u: ordered[:, r, g, u, :]
-
-        def unsorted_wh(j):
-            raw = wh_raw[j][:].bitcast(F32)
-            return lambda r, g, u: raw[:, r, word_columns(g, u)]
 
         def transpose_wh(words, copies):
             grouped = wh_stage.tile([P, PASSES, CHUNK, PACK], BF16, name="wh_grouped", align_bytes=64)
@@ -178,7 +190,7 @@ def tile_compute_gate_e_kernel(tc, input_word, hidden_states, Wx_words, Wx_scale
             return codes, planes
 
         def spread_bias():
-            spread = flip_banks.tile([P, SLABS, CHUNK], BF16, name="spread", tag="bank")
+            spread = sum_banks.tile([P, SLABS, CHUNK], BF16, name="spread", tag="sums")
             for row in range(SLABS):
                 nc.tensor.matmul(
                     spread[:, row, :],
@@ -187,7 +199,7 @@ def tile_compute_gate_e_kernel(tc, input_word, hidden_states, Wx_words, Wx_scale
                     start=True,
                     stop=True,
                 )
-            nc.scalar.copy(out=bias_all[:, 0, 0:HID].rearrange("p (s n) -> p s n", n=CHUNK), in_=spread[:])
+            nc.vector.tensor_copy(out=bias_all[:, 0, 0:HID].rearrange("p (s n) -> p s n", n=CHUNK), in_=spread[:])
 
         def input_passes(bank, j, bt, cols):
             cell, n0 = chunks[j][2], chunks[j][4]
@@ -214,16 +226,19 @@ def tile_compute_gate_e_kernel(tc, input_word, hidden_states, Wx_words, Wx_scale
                     stop=(g == PASSES - 1),
                 )
 
-        def finish(bank, j, bt, cols):
-            func, out, cell, out_col, n0 = chunks[j]
-            width = cols.stop - cols.start
-            result = results.tile([P, width], F32, name="result")
+        def add_bias(bank, j, cols):
+            cell, n0 = chunks[j][2], chunks[j][4]
+            result = results.tile([P, cols.stop - cols.start], F32, name="result")
             nc.vector.tensor_tensor(
                 out=result[:],
                 in0=bank[:, cols],
                 in1=bias_all[:, cell, n0 + cols.start : n0 + cols.stop],
                 op=mybir.AluOpType.add,
             )
+            return result
+
+        def finish(result, j, bt, cols):
+            func, out, cell, out_col = chunks[j][:4]
             nc.scalar.activation(out=result[:], in_=result[:], func=func)
             nc.sync.dma_start(
                 out=out[P * bt : P * (bt + 1), cell, out_col + cols.start : out_col + cols.stop], in_=result[:]
@@ -232,7 +247,7 @@ def tile_compute_gate_e_kernel(tc, input_word, hidden_states, Wx_words, Wx_scale
         def open_sums(j, batch_tiles):
             sums = []
             for bt in batch_tiles:
-                bank = sum_banks.tile([P, CHUNK], F32, name="sums")
+                bank = sum_banks.tile([P, CHUNK], F32, name="sums", tag="sums")
                 input_passes(bank, j, bt, ALL_COLS)
                 sums.append(bank)
             return sums
@@ -240,39 +255,46 @@ def tile_compute_gate_e_kernel(tc, input_word, hidden_states, Wx_words, Wx_scale
         def close_sums(j, sums, codes, planes):
             for bt, bank in enumerate(sums):
                 hidden_passes(bank, bt, ALL_COLS, codes, planes)
-            for bt, bank in enumerate(sums):
-                finish(bank, j, bt, ALL_COLS)
+            return [add_bias(bank, j, ALL_COLS) for bank in sums]
+
+        def finish_chunk(sums, j):
+            for bt, result in enumerate(sums):
+                finish(result, j, bt, ALL_COLS)
 
         on_scalar, on_vector = nc.scalar.copy, nc.vector.tensor_copy
         x_codes, x_planes = quantise_activations(
-            transpose_activations(x_raw, "x", (on_scalar, on_vector, on_scalar, on_scalar)), "x"
+            transpose_activations([unsorted_activations(raw) for raw in x_raw], "x", (on_scalar, on_vector, on_scalar, on_scalar)), "x"
         )
-        ordered = sort_wh(0)
+        spread_bias()
+        ordered = sort_wh(0, on_vector)
+        h_words = [sort_activations(h_raw[bt], "h_ordered%d" % bt) for bt in range(B_TILES - 1)]
+        h_words.append(unsorted_activations(h_raw[B_TILES - 1]))
         sums = open_sums(0, range(B_TILES))
         wh_grouped = {0: transpose_wh(ordered, (on_scalar, on_vector) * 2)}
-        h_staged = transpose_activations(h_raw, "h", (on_scalar,) * 4)
-        spread_bias()
+        h_staged = transpose_activations(h_words, "h", (on_scalar,) * 4)
         codes, planes = quantise_wh(wh_grouped[0])
         h_codes, h_planes = quantise_activations(h_staged, "h")
-        wh_ordered = {}
-        close_sums(0, sums, codes, planes)
-        wh_grouped[1] = transpose_wh(unsorted_wh(1), (on_vector, on_scalar) * 2)
+        wh_ordered = {1: sort_wh(1, on_scalar)}
+        biased = close_sums(0, sums, codes, planes)
+        wh_grouped[1] = transpose_wh(wh_ordered[1], (on_vector, on_scalar) * 2)
+        finish_chunk(biased, 0)
         codes, planes = quantise_wh(wh_grouped[1])
+        wh_ordered[2] = sort_wh(2, on_vector)
         sums = open_sums(1, range(B_TILES))
-        wh_grouped[2] = transpose_wh(unsorted_wh(2), (on_scalar,) * 4)
-        wh_ordered[3] = sort_wh(3)
+        wh_grouped[2] = transpose_wh(wh_ordered[2], (on_scalar,) * 4)
+        wh_ordered[3] = sort_wh(3, on_vector)
         for j in range(1, n_chunks):
-            close_sums(j, sums, codes, planes)
+            finish_chunk(close_sums(j, sums, codes, planes), j)
             if j + 1 < n_chunks:
                 codes, planes = quantise_wh(wh_grouped[j + 1])
             if j + 2 < n_chunks:
                 wh_grouped[j + 2] = transpose_wh(wh_ordered[j + 2], (on_scalar,) * 4)
             if j + 3 < n_chunks:
-                wh_ordered[j + 3] = sort_wh(j + 3)
+                wh_ordered[j + 3] = sort_wh(j + 3, on_vector)
             if j + 1 < n_chunks:
                 sums = open_sums(j + 1, range(B_TILES if j + 2 < n_chunks else B_TILES - 1))
         for cols in END_PIECES:
             bank = flip_banks.tile([P, CHUNK], F32, name="end_sums", tag="bank")
             input_passes(bank, n_chunks - 1, B_TILES - 1, cols)
             hidden_passes(bank, B_TILES - 1, cols, codes, planes)
-            finish(bank, n_chunks - 1, B_TILES - 1, cols)
+            finish(add_bias(bank, n_chunks - 1, cols), n_chunks - 1, B_TILES - 1, cols)

@@ -53,6 +53,8 @@ def tile_compute_gate_e_kernel(tc, input_word, hidden_states, Wx_words, Wx_scale
         sum_banks = ctx.enter_context(tc.psum_pool(name="sum_banks", bufs=B_TILES))
         ctx.enter_context(tc.manual_schedule())
 
+        zeros = keep.tile([P, CHUNK], BF16, name="zeros")
+        nc.vector.memset(zeros[:].bitcast(I32), 0)
         wx_planes = keep.tile([P, 2 * HID], U8, name="wx_planes", align_bytes=64)
         nc.vector.memset(wx_planes[:].bitcast(I32), 0)
         warm = keep.tile([P, 1], F32, name="warm")
@@ -100,9 +102,9 @@ def tile_compute_gate_e_kernel(tc, input_word, hidden_states, Wx_words, Wx_scale
                 out=wx_planes[32 * quadrant : 32 * quadrant + 16, :].bitcast(I32),
                 in_=Wx_scales[:, 4 * quadrant : 4 * quadrant + 4, :].bitcast(I32),
             )
-        wx_words = [load_wx(0)]
-        wh_raw = [load_wh(0)]
         h_raw = load_activations(hidden_states, "h")
+        wh_raw = [load_wh(0)]
+        wx_words = [load_wx(0)]
         wh_raw.append(load_wh(1))
         wx_words.append(load_wx(1))
         wh_raw.append(load_wh(2))
@@ -117,24 +119,19 @@ def tile_compute_gate_e_kernel(tc, input_word, hidden_states, Wx_words, Wx_scale
         def word_columns(g, u):
             return slice(PASS_WORDS * g + u, PASS_WORDS * (g + 1), PAIR)
 
-        def sort_activations(raw, name):
-            ordered = keep.tile([P, PASSES, PAIR, P], F32, name=name)
-            nc.vector.tensor_copy(
-                out=ordered[:], in_=raw[:].bitcast(F32).rearrange("p (g w u) -> p g u w", g=PASSES, u=PAIR)
-            )
-            return lambda g, u: ordered[:, g, u, :]
+        def keep_busy(count):
+            idle = sum_banks.tile([P, CHUNK], F32, name="idle", tag="sums")
+            for repeat in range(count):
+                nc.tensor.matmul(idle[:], lhsT=zeros[:, 0:P], rhs=zeros[:], start=True, stop=True)
 
-        def unsorted_activations(raw):
-            words = raw[:].bitcast(F32)
-            return lambda g, u: words[:, word_columns(g, u)]
-
-        def transpose_activations(words, name, copies):
+        def transpose_activations(raw, name, copies):
             staged = []
             for bt in range(B_TILES):
+                words = raw[bt][:].bitcast(F32)
                 flipped = flip_banks.tile([P, PASSES, PAIR, P], F32, name="flipped", tag="bank")
                 for g in range(PASSES):
                     for u in range(PAIR):
-                        nc.tensor.transpose(flipped[:, g, u, :], words[bt](g, u), ident_f32[:])
+                        nc.tensor.transpose(flipped[:, g, u, :], words[:, word_columns(g, u)], ident_f32[:])
                 grouped = keep.tile([P, PASSES, P, PACK], BF16, name="%s_grouped%d" % (name, bt), align_bytes=64)
                 copies[bt](out=grouped[:].bitcast(F32), in_=flipped[:].rearrange("p g u b -> p g b u"))
                 staged.append(grouped)
@@ -151,15 +148,19 @@ def tile_compute_gate_e_kernel(tc, input_word, hidden_states, Wx_words, Wx_scale
                 )
             return codes, planes
 
-        def sort_wh(j, copy):
+        def sort_wh(j, first_copy, second_copy):
             raw = wh_raw[j][:].bitcast(F32)
             ordered = wh_order.tile([P, ROWS, PASSES, PAIR, P], F32, name="wh_ordered")
-            for first in range(0, ROWS, PAIR):
+            for first, copy in ((0, first_copy), (PAIR, second_copy)):
                 copy(
                     out=ordered[:, first : first + PAIR].rearrange("p r g u w -> p (r g) u w"),
                     in_=raw[:, first : first + PAIR, :].rearrange("p r (g w u) -> p (r g) u w", g=PASSES, u=PAIR),
                 )
             return lambda r, g, u: ordered[:, r, g, u, :]
+
+        def unsorted_wh(j):
+            raw = wh_raw[j][:].bitcast(F32)
+            return lambda r, g, u: raw[:, r, word_columns(g, u)]
 
         def transpose_wh(words, copies):
             grouped = wh_stage.tile([P, PASSES, CHUNK, PACK], BF16, name="wh_grouped", align_bytes=64)
@@ -262,27 +263,25 @@ def tile_compute_gate_e_kernel(tc, input_word, hidden_states, Wx_words, Wx_scale
                 finish(result, j, bt, ALL_COLS)
 
         on_scalar, on_vector = nc.scalar.copy, nc.vector.tensor_copy
-        x_codes, x_planes = quantise_activations(
-            transpose_activations([unsorted_activations(raw) for raw in x_raw], "x", (on_scalar, on_vector, on_scalar, on_scalar)), "x"
-        )
+        keep_busy(4)
+        x_staged = transpose_activations(x_raw, "x", (on_scalar, on_vector) * 2)
+        x_codes, x_planes = quantise_activations(x_staged, "x")
         spread_bias()
-        ordered = sort_wh(0, on_vector)
-        h_words = [sort_activations(h_raw[bt], "h_ordered%d" % bt) for bt in range(B_TILES - 1)]
-        h_words.append(unsorted_activations(h_raw[B_TILES - 1]))
-        sums = open_sums(0, range(B_TILES))
-        wh_grouped = {0: transpose_wh(ordered, (on_scalar, on_vector) * 2)}
-        h_staged = transpose_activations(h_words, "h", (on_scalar,) * 4)
-        codes, planes = quantise_wh(wh_grouped[0])
+        h_staged = transpose_activations(h_raw, "h", (on_scalar, on_vector) * 2)
         h_codes, h_planes = quantise_activations(h_staged, "h")
-        wh_ordered = {1: sort_wh(1, on_scalar)}
+        keep_busy(2)
+        wh_grouped = {0: transpose_wh(unsorted_wh(0), (on_scalar, on_vector) * 2)}
+        codes, planes = quantise_wh(wh_grouped[0])
+        sums = open_sums(0, range(B_TILES))
+        wh_ordered = {1: sort_wh(1, on_scalar, on_scalar)}
         biased = close_sums(0, sums, codes, planes)
         wh_grouped[1] = transpose_wh(wh_ordered[1], (on_vector, on_scalar) * 2)
-        finish_chunk(biased, 0)
         codes, planes = quantise_wh(wh_grouped[1])
-        wh_ordered[2] = sort_wh(2, on_vector)
+        wh_ordered[2] = sort_wh(2, on_scalar, on_vector)
+        finish_chunk(biased, 0)
         sums = open_sums(1, range(B_TILES))
         wh_grouped[2] = transpose_wh(wh_ordered[2], (on_scalar,) * 4)
-        wh_ordered[3] = sort_wh(3, on_vector)
+        wh_ordered[3] = sort_wh(3, on_vector, on_vector)
         for j in range(1, n_chunks):
             finish_chunk(close_sums(j, sums, codes, planes), j)
             if j + 1 < n_chunks:
@@ -290,7 +289,7 @@ def tile_compute_gate_e_kernel(tc, input_word, hidden_states, Wx_words, Wx_scale
             if j + 2 < n_chunks:
                 wh_grouped[j + 2] = transpose_wh(wh_ordered[j + 2], (on_scalar,) * 4)
             if j + 3 < n_chunks:
-                wh_ordered[j + 3] = sort_wh(j + 3, on_vector)
+                wh_ordered[j + 3] = sort_wh(j + 3, on_vector, on_vector)
             if j + 1 < n_chunks:
                 sums = open_sums(j + 1, range(B_TILES if j + 2 < n_chunks else B_TILES - 1))
         for cols in END_PIECES:

from contextlib import ExitStack

import concourse.mybir as mybir
from concourse.masks import make_identity

F32 = mybir.dt.float32
BF16 = mybir.dt.bfloat16
I32 = mybir.dt.int32
U32 = mybir.dt.uint32
U8 = mybir.dt.uint8
FP8X4 = mybir.dt.float8_e4m3fn_x4
ACT = mybir.ActivationFunctionType

P = 128
PACK = 4
PAIR = 2
K_PASS = P * PACK
BATCH = 512
K = 1024
HID = 1024
CELLS = 2
PASSES = K // K_PASS
PASS_WORDS = K_PASS // PAIR
B_TILES = BATCH // P
CHUNK = 512
SLABS = HID // CHUNK
ROWS = CHUNK // P
ALL_COLS = slice(0, CHUNK)
END_PIECES = (slice(0, 256), slice(256, 384), slice(384, 512))
BIAS_BEHIND = 3
RESULT_BUFS = 20

FLOPS = 2 * BATCH * (CELLS * 2 * HID) * (2 * K)


def tile_compute_gate_e_kernel(tc, input_word, hidden_states, Wx_words, Wx_scales, bx, Wh, out_0, out_1):
    nc = tc.nc

    chunks = []
    for func, out, first_n in ((ACT.Sigmoid, out_1, 0), (ACT.Tanh, out_0, HID)):
        for cell in range(CELLS):
            for slab in range(SLABS):
                chunks.append((func, out, cell, slab * CHUNK, first_n + slab * CHUNK))
    n_chunks = len(chunks)

    with ExitStack() as ctx:
        keep = ctx.enter_context(tc.tile_pool(name="keep", bufs=1))
        wh_rows = ctx.enter_context(tc.tile_pool(name="wh_rows", bufs=6))
        wh_order = ctx.enter_context(tc.tile_pool(name="wh_order", bufs=3))
        wh_stage = ctx.enter_context(tc.tile_pool(name="wh_stage", bufs=2))
        results = ctx.enter_context(tc.tile_pool(name="results", bufs=RESULT_BUFS))
        flip_banks = ctx.enter_context(tc.psum_pool(name="flip_banks", bufs=4))
        sum_banks = ctx.enter_context(tc.psum_pool(name="sum_banks", bufs=B_TILES))
        ctx.enter_context(tc.manual_schedule())

        zeros = keep.tile([P, CHUNK], BF16, name="zeros")
        nc.vector.memset(zeros[:].bitcast(I32), 0)
        wx_planes = keep.tile([P, 2 * HID], U8, name="wx_planes", align_bytes=64)
        nc.vector.memset(wx_planes[:].bitcast(I32), 0)
        warm = keep.tile([P, 1], F32, name="warm")
        nc.vector.memset(warm[:], 0.0)
        nc.scalar.activation(out=warm[:], in_=warm[:], func=ACT.Sigmoid)
        bias_rows = keep.tile([P, CHUNK], BF16, name="bias_rows")
        nc.vector.memset(bias_rows[:].bitcast(I32), 0)
        ident_bf16 = keep.tile([P, P], BF16, name="ident_bf16")
        ident_f32 = keep.tile([P, P], F32, name="ident_f32")
        make_identity(nc, ident_f32[:])
        make_identity(nc, ident_bf16[:])

        def load_activations(rows, name):
            tiles = []
            for bt in range(B_TILES):
                raw = keep.tile([P, K], BF16, name="%s_raw%d" % (name, bt))
                nc.sync.dma_start(out=raw[:], in_=rows[P * bt : P * (bt + 1), :])
                tiles.append(raw)
            return tiles

        def load_wx(j):
            cell, n0 = chunks[j][2], chunks[j][4]
            words = keep.tile([P, PASSES, CHUNK], U32, name="wx_words%d" % j, align_bytes=64)
            nc.sync.dma_start(
                out=words[:].bitcast(I32),
                in_=Wx_words[PASSES * cell : PASSES * (cell + 1), :, n0 : n0 + CHUNK, :]
                .rearrange("g p n t -> p g (n t)")
                .bitcast(I32),
            )
            return words

        def load_wh(j):
            cell, n0 = chunks[j][2], chunks[j][4]
            raw = wh_rows.tile([P, ROWS, K], BF16, name="wh_raw")
            rows = Wh[cell, n0 : n0 + CHUNK, :].rearrange("(q r) k -> q r k", r=ROWS)
            for first in range(0, ROWS, PAIR):
                nc.sync.dma_start(out=raw[:, first : first + PAIR, :], in_=rows[:, first : first + PAIR, :])
            return raw

        bias_all = keep.tile([P, CELLS, 2 * HID], BF16, name="bias_all")
        x_raw = load_activations(input_word, "x")
        nc.sync.dma_start(out=bias_rows[0:SLABS, :], in_=bx[0, 0:HID].rearrange("(s n) -> s n", n=CHUNK))
        for quadrant in range(4):
            nc.sync.dma_start(
                out=wx_planes[32 * quadrant : 32 * quadrant + 16, :].bitcast(I32),
                in_=Wx_scales[:, 4 * quadrant : 4 * quadrant + 4, :].bitcast(I32),
            )
        h_raw = load_activations(hidden_states, "h")
        wh_raw = [load_wh(0)]
        wx_words = [load_wx(0)]
        wh_raw.append(load_wh(1))
        wx_words.append(load_wx(1))
        wh_raw.append(load_wh(2))
        for j in range(2, n_chunks):
            if j + 1 < n_chunks:
                wh_raw.append(load_wh(j + 1))
            wx_words.append(load_wx(j))
            if j == BIAS_BEHIND:
                nc.sync.dma_start(out=bias_all[:, 1, 0:HID], in_=bx[1, 0:HID].partition_broadcast(P))
        nc.sync.dma_start(out=bias_all[:, :, HID : 2 * HID], in_=bx[:, HID : 2 * HID].partition_broadcast(P))

        def word_columns(g, u):
            return slice(PASS_WORDS * g + u, PASS_WORDS * (g + 1), PAIR)

        def keep_busy(count):
            idle = sum_banks.tile([P, CHUNK], F32, name="idle", tag="sums")
            for repeat in range(count):
                nc.tensor.matmul(idle[:], lhsT=zeros[:, 0:P], rhs=zeros[:], start=True, stop=True)

        def transpose_activations(raw, name, copies):
            staged = []
            for bt in range(B_TILES):
                words = raw[bt][:].bitcast(F32)
                flipped = flip_banks.tile([P, PASSES, PAIR, P], F32, name="flipped", tag="bank")
                for g in range(PASSES):
                    for u in range(PAIR):
                        nc.tensor.transpose(flipped[:, g, u, :], words[:, word_columns(g, u)], ident_f32[:])
                grouped = keep.tile([P, PASSES, P, PACK], BF16, name="%s_grouped%d" % (name, bt), align_bytes=64)
                copies[bt](out=grouped[:].bitcast(F32), in_=flipped[:].rearrange("p g u b -> p g b u"))
                staged.append(grouped)
            return staged

        def quantise_activations(staged, name):
            codes = keep.tile([P, B_TILES, PASSES * P], U32, name="%s_codes" % name, align_bytes=64)
            planes = keep.tile([P, B_TILES, PASSES * P], U8, name="%s_planes" % name, align_bytes=64)
            for bt in range(B_TILES):
                nc.vector.quantize_mx(
                    out=codes[:, bt, :].bitcast(FP8X4),
                    scales=planes[:, bt, :],
                    in_=staged[bt][:].rearrange("p g b t -> p (g b t)"),
                )
            return codes, planes

        def sort_wh(j, first_copy, second_copy):
            raw = wh_raw[j][:].bitcast(F32)
            ordered = wh_order.tile([P, ROWS, PASSES, PAIR, P], F32, name="wh_ordered")
            for first, copy in ((0, first_copy), (PAIR, second_copy)):
                copy(
                    out=ordered[:, first : first + PAIR].rearrange("p r g u w -> p (r g) u w"),
                    in_=raw[:, first : first + PAIR, :].rearrange("p r (g w u) -> p (r g) u w", g=PASSES, u=PAIR),
                )
            return lambda r, g, u: ordered[:, r, g, u, :]

        def unsorted_wh(j):
            raw = wh_raw[j][:].bitcast(F32)
            return lambda r, g, u: raw[:, r, word_columns(g, u)]

        def transpose_wh(words, copies):
            grouped = wh_stage.tile([P, PASSES, CHUNK, PACK], BF16, name="wh_grouped", align_bytes=64)
            copies = list(copies)
            for first in range(0, ROWS, PAIR):
                for g in range(PASSES):
                    flipped = flip_banks.tile([P, PAIR, PAIR, P], F32, name="flipped", tag="bank")
                    for r in range(PAIR):
                        for u in range(PAIR):
                            nc.tensor.transpose(flipped[:, r, u, :], words(first + r, g, u), ident_f32[:])
                    copies.pop(0)(
                        out=grouped[:, g].bitcast(F32).rearrange("p (q r) u -> p q r u", r=ROWS)[
                            :, :, first : first + PAIR, :
                        ],
                        in_=flipped[:].rearrange("p r u q -> p q r u"),
                    )
            return grouped

        def quantise_wh(grouped):
            codes = wh_stage.tile([P, PASSES, CHUNK], U32, name="wh_codes", align_bytes=64)
            planes = wh_stage.tile([P, PASSES, CHUNK], U8, name="wh_planes", align_bytes=64)
            for g in range(PASSES):
                nc.vector.quantize_mx(
                    out=codes[:, g, :].bitcast(FP8X4),
                    scales=planes[:, g, :],
                    in_=grouped[:, g].rearrange("p n t -> p (n t)"),
                )
            return codes, planes

        def spread_bias():
            spread = sum_banks.tile([P, SLABS, CHUNK], BF16, name="spread", tag="sums")
            for row in range(SLABS):
                nc.tensor.matmul(
                    spread[:, row, :],
                    lhsT=ident_bf16[:, row : row + 1].to_broadcast([P, P]),
                    rhs=bias_rows[:],
                    start=True,
                    stop=True,
                )
            nc.vector.tensor_copy(out=bias_all[:, 0, 0:HID].rearrange("p (s n) -> p s n", n=CHUNK), in_=spread[:])

        def input_passes(bank, j, bt, cols):
            cell, n0 = chunks[j][2], chunks[j][4]
            for g in range(PASSES):
                nc.tensor.matmul_mx(
                    out=bank[:, cols],
                    lhsT=x_codes[:, bt, P * g : P * (g + 1)].bitcast(FP8X4),
                    lhsT_scale=x_planes[:, bt, P * g : P * (g + 1)],
                    rhs=wx_words[j][:, g, cols].bitcast(FP8X4),
                    rhs_scale=wx_planes[4 * (PASSES * cell + g) : P, n0 + cols.start : n0 + cols.stop],
                    start=(g == 0),
                    stop=False,
                )

        def hidden_passes(bank, bt, cols, codes, planes):
            for g in range(PASSES):
                nc.tensor.matmul_mx(
                    out=bank[:, cols],
                    lhsT=h_codes[:, bt, P * g : P * (g + 1)].bitcast(FP8X4),
                    lhsT_scale=h_planes[:, bt, P * g : P * (g + 1)],
                    rhs=codes[:, g, cols].bitcast(FP8X4),
                    rhs_scale=planes[:, g, cols],
                    start=False,
                    stop=(g == PASSES - 1),
                )

        def add_bias(bank, j, cols):
            cell, n0 = chunks[j][2], chunks[j][4]
            result = results.tile([P, cols.stop - cols.start], F32, name="result")
            nc.vector.tensor_tensor(
                out=result[:],
                in0=bank[:, cols],
                in1=bias_all[:, cell, n0 + cols.start : n0 + cols.stop],
                op=mybir.AluOpType.add,
            )
            return result

        def finish(result, j, bt, cols):
            func, out, cell, out_col = chunks[j][:4]
            nc.scalar.activation(out=result[:], in_=result[:], func=func)
            nc.sync.dma_start(
                out=out[P * bt : P * (bt + 1), cell, out_col + cols.start : out_col + cols.stop], in_=result[:]
            )

        def open_sums(j, batch_tiles):
            sums = []
            for bt in batch_tiles:
                bank = sum_banks.tile([P, CHUNK], F32, name="sums", tag="sums")
                input_passes(bank, j, bt, ALL_COLS)
                sums.append(bank)
            return sums

        def close_sums(j, sums, codes, planes):
            for bt, bank in enumerate(sums):
                hidden_passes(bank, bt, ALL_COLS, codes, planes)
            return [add_bias(bank, j, ALL_COLS) for bank in sums]

        def finish_chunk(sums, j):
            for bt, result in enumerate(sums):
                finish(result, j, bt, ALL_COLS)

        on_scalar, on_vector = nc.scalar.copy, nc.vector.tensor_copy
        keep_busy(4)
        x_staged = transpose_activations(x_raw, "x", (on_scalar, on_vector) * 2)
        x_codes, x_planes = quantise_activations(x_staged, "x")
        spread_bias()
        h_staged = transpose_activations(h_raw, "h", (on_scalar, on_vector) * 2)
        h_codes, h_planes = quantise_activations(h_staged, "h")
        keep_busy(2)
        wh_grouped = {0: transpose_wh(unsorted_wh(0), (on_scalar, on_vector) * 2)}
        codes, planes = quantise_wh(wh_grouped[0])
        sums = open_sums(0, range(B_TILES))
        wh_ordered = {1: sort_wh(1, on_scalar, on_scalar)}
        biased = close_sums(0, sums, codes, planes)
        wh_grouped[1] = transpose_wh(wh_ordered[1], (on_vector, on_scalar) * 2)
        codes, planes = quantise_wh(wh_grouped[1])
        wh_ordered[2] = sort_wh(2, on_scalar, on_vector)
        finish_chunk(biased, 0)
        sums = open_sums(1, range(B_TILES))
        wh_grouped[2] = transpose_wh(wh_ordered[2], (on_scalar,) * 4)
        wh_ordered[3] = sort_wh(3, on_vector, on_vector)
        for j in range(1, n_chunks):
            finish_chunk(close_sums(j, sums, codes, planes), j)
            if j + 1 < n_chunks:
                codes, planes = quantise_wh(wh_grouped[j + 1])
            if j + 2 < n_chunks:
                wh_grouped[j + 2] = transpose_wh(wh_ordered[j + 2], (on_scalar,) * 4)
            if j + 3 < n_chunks:
                wh_ordered[j + 3] = sort_wh(j + 3, on_vector, on_vector)
            if j + 1 < n_chunks:
                sums = open_sums(j + 1, range(B_TILES if j + 2 < n_chunks else B_TILES - 1))
        for cols in END_PIECES:
            bank = flip_banks.tile([P, CHUNK], F32, name="end_sums", tag="bank")
            input_passes(bank, n_chunks - 1, B_TILES - 1, cols)
            hidden_passes(bank, B_TILES - 1, cols, codes, planes)
            finish(add_bias(bank, n_chunks - 1, cols), n_chunks - 1, B_TILES - 1, cols)
